import numpy as np
import ml_dtypes


def mxq(x, axis, fmt="e4m3"):
    dtype, down = {"e4m3": (ml_dtypes.float8_e4m3fn, 7), "e5m2": (ml_dtypes.float8_e5m2, 14)}[fmt]
    v = np.moveaxis(np.asarray(x, np.float32).astype(ml_dtypes.bfloat16).astype(np.float64), axis, -1)
    blocks = v.reshape(v.shape[:-1] + (-1, 32))
    amax = np.abs(blocks).max(-1, keepdims=True)
    byte = np.maximum(np.where(amax > 0, np.frexp(amax)[1] - 1 + 127, 0) - down, 1)
    scale = np.exp2(byte - 127.0)
    codes = (blocks / scale).astype(np.float32).astype(dtype).astype(np.float64)
    return np.moveaxis((codes * scale).reshape(v.shape), -1, axis)


WIDE = False


def mx_kscale(k):
    if not WIDE:
        return np.ones(k)
    levels = np.array([10, -10, 5, -5, 0])
    if k % 512:
        return np.exp2(np.random.permutation(np.resize(levels, k // 32))).repeat(32)
    a = np.empty((k // 512, 16))
    for p in range(k // 512):
        a[p, :8] = np.random.permutation(np.resize(levels, 8))
        for g in range(8):
            far = levels[np.abs(levels - a[p, g]) >= 10]
            a[p, g + 8] = far[np.random.randint(len(far))]
    return np.exp2(a.ravel()).repeat(32)


BF16 = ml_dtypes.bfloat16


def bf(x):
    return np.asarray(x, np.float32).astype(BF16)


def f64(x):
    return np.asarray(x).astype(np.float64)


B, N, L, H, S, R, C = 4, 1024, 4, 64, 2, 2, 512


def setup_inputs():
    s = mx_kscale(N)
    return {"x": bf(np.random.standard_normal((B, N, L, H)) * s[None, :, None, None]),
            "support": bf(np.random.standard_normal((S, N, N)) * 0.6 / np.sqrt(N) * s[:, None] / s[None, :]),
            "eps": bf(np.random.uniform(0.1, 0.3, (1,)))}


def reference(x, support, eps):
    xv = f64(x).reshape(B, N, L * H)
    sup = f64(support)
    g = 1.0 + f64(eps)
    xq = mxq(xv, 1, "e4m3")
    res = []
    for i in range(S):
        aq = mxq(sup[i], 1, "e4m3")
        out, oq = xv, xq
        for j in range(R):
            out = g * out + (aq @ oq)
            res.append(out)
            if j + 1 < R:
                oq = mxq(out, 1, "e4m3")
    return np.stack(res, axis=-1).reshape(B, N, L, H * len(res))

@@ -1,0 +1,353 @@
+from contextlib import ExitStack
+
+import concourse.mybir as mybir
+from concourse.masks import make_identity
+
+F32 = mybir.dt.float32
+BF16 = mybir.dt.bfloat16
+U32 = mybir.dt.uint32
+U8 = mybir.dt.uint8
+FP8X4 = mybir.dt.float8_e4m3fn_x4
+MULT = mybir.AluOpType.mult
+ADD = mybir.AluOpType.add
+
+P = 128
+B = 4
+D = 256
+S = 2
+NT = 8
+FLOPS = 4 * 2 * 1024 * 1024 * 1024
+
+MANUAL = False
+DEFER_H = 2
+PRE = 1
+X_ENG = ["v", "s", "s", "s"]
+R_ENG = ["ss", "sg", "gs", "sg", "gs", "gg", "gs", "vs"]
+ILV = ["sg", "gs", "sg", "sg", "sv", "gs", "ss", "ss", "sg", "sg", "ss", "sv", "sv", "gs", "sv", "sg"]
+E_ENG = ["vv", "ss", "vs", "ss", "sv", "ss", "ss", "sv"]
+G_SPLIT = 2
+EPS_MM = True
+X_FIRST = 1
+XG_BUFS = 2
+SPLIT_STORES = 0
+E_LAST = ["s", "s"]
+XR2_AT = 0
+XR3_AT = 4
+XQ2_AT = 0
+XQ3_AT = 4
+RATES = [1, 1, 1, 3, 0, 1, 0, 0, 0, 1, 3, 0, 0, 1, 0, 0]
+HH_BUFS = 6
+O_BUFS = 4
+
+
+def tile_ginconvfft_pa_t_kernel(tc, x, support, eps, out):
+    nc = tc.nc
+    with ExitStack() as ctx:
+        keep = ctx.enter_context(tc.tile_pool(name="keep", bufs=1))
+        atg_pool = ctx.enter_context(tc.tile_pool(name="atg", bufs=4))
+        xg_pool = ctx.enter_context(tc.tile_pool(name="xg", bufs=XG_BUFS))
+        hh_pool = ctx.enter_context(tc.tile_pool(name="hh", bufs=HH_BUFS))
+        hg_pool = ctx.enter_context(tc.tile_pool(name="hg", bufs=3))
+        hc_pool = ctx.enter_context(tc.tile_pool(name="hc", bufs=6))
+        o_pool = ctx.enter_context(tc.tile_pool(name="o", bufs=O_BUFS))
+        psum = ctx.enter_context(tc.psum_pool(name="psum", bufs=8))
+        if MANUAL:
+            ctx.enter_context(tc.manual_schedule())
+
+        def copy(eng, dst, src):
+            if eng == "v":
+                nc.vector.tensor_copy(out=dst, in_=src)
+            elif eng == "s":
+                nc.scalar.copy(out=dst, in_=src)
+            else:
+                n = dst.shape[1] // G_SPLIT
+                for i in range(G_SPLIT):
+                    nc.gpsimd.tensor_scalar(
+                        out=dst[:, i * n : (i + 1) * n],
+                        in0=src[:, i * n : (i + 1) * n],
+                        scalar1=1.0,
+                        scalar2=0.0,
+                        op0=MULT,
+                        op1=ADD,
+                    )
+
+        ident = keep.tile([P, P], F32, name="ident")
+        make_identity(nc, ident[:])
+        gain = keep.tile([P, 1], F32, name="gain")
+        if EPS_MM:
+            eps_row = keep.tile([P, 32], BF16, name="eps_row")
+            nc.vector.memset(eps_row[:], 0.0)
+            ones = keep.tile([P, P], BF16, name="ones")
+            nc.vector.memset(ones[:], 1.0)
+            nc.scalar.dma_start(out=eps_row[0:1, 0:1], in_=eps.rearrange("(o n) -> o n", o=1))
+            eps_bank = psum.tile([P, 512], F32, name="bank", tag="bank")
+            nc.tensor.matmul(out=eps_bank[:, 0:32], lhsT=ones[:], rhs=eps_row[:], start=True, stop=True)
+            nc.vector.tensor_scalar_add(out=gain[:], in0=eps_bank[:, 0:1], scalar1=1.0)
+        else:
+            eps_sb = keep.tile([P, 1], BF16, name="eps_sb")
+            nc.scalar.dma_start(out=eps_sb[:], in_=eps.partition_broadcast(P))
+            nc.vector.tensor_scalar_add(out=gain[:], in0=eps_sb[:], scalar1=1.0)
+
+        x_raw = {}
+        a_raw = {}
+
+        def load_x(b):
+            t = keep.tile([P, NT, D], BF16, name="x_raw%d" % b)
+            nc.sync.dma_start(
+                out=t[:].rearrange("p (g t) d -> p g (t d)", t=4),
+                in_=x[b].rearrange("(g p t) l h -> p g (t l h)", g=2, p=P, t=4),
+            )
+            x_raw[b] = t
+
+        def load_a(s, gu):
+            if (gu // 2) not in a_raw:
+                a_raw[gu // 2] = hh_pool.tile([P, 4, 2048], BF16, name="a_raw", tag="hh")
+            nc.sync.dma_start(
+                out=a_raw[gu // 2][:, 2 * (gu % 2) + s, :],
+                in_=support[s, 512 * (gu // 2) : 512 * (gu // 2 + 1), :].rearrange("(p h e) m -> h p (e m)", h=2, e=2)[gu % 2],
+            )
+
+        for b in range(X_FIRST):
+            load_x(b)
+        for gu in range(4):
+            for s in range(S):
+                load_a(s, gu)
+        for b in range(X_FIRST, B):
+            load_x(b)
+
+        x_grp = {}
+        x_codes = {}
+        x_scales = {}
+
+        def regroup_x(b):
+            t = xg_pool.tile([P, 2, D, 4], BF16, name="x_grp", align_bytes=64)
+            for g in range(2):
+                copy(X_ENG[b], t[:, g, :, :], x_raw[b][:, 4 * g : 4 * (g + 1), :].rearrange("p t d -> p d t"))
+            x_grp[b] = t
+
+        def quant_x(b):
+            c = keep.tile([P, 512], U32, name="x_codes%d" % b, align_bytes=64)
+            sc = keep.tile([P, 512], U8, name="x_scales%d" % b, align_bytes=64)
+            nc.vector.quantize_mx(
+                out=c[:].bitcast(FP8X4), scales=sc[:], in_=x_grp[b][:].rearrange("p g d t -> p (g d t)")
+            )
+            x_codes[b] = c
+            x_scales[b] = sc
+
+        at_grp = {}
+        at_codes = {}
+        at_scales = {}
+
+        def transpose_a(s, gu, engs):
+            a32 = a_raw[gu // 2][:, 2 * (gu % 2) + s, :].bitcast(F32)
+            grp = atg_pool.tile([P, 2048], BF16, name="at_grp", align_bytes=64)
+            g32 = grp[:].bitcast(F32)
+            banks = []
+            for g in range(2):
+                bank = psum.tile([P, 512], F32, name="bank", tag="bank")
+                for u in range(2):
+                    for e in range(2):
+                        w0 = 512 * e + 256 * g
+                        nc.tensor.transpose(
+                            out=bank[:, 256 * u + 128 * e : 256 * u + 128 * (e + 1)],
+                            in_=a32[:, w0 + u : w0 + 256 : 2],
+                            identity=ident[:],
+                        )
+                banks.append(bank)
+            for g in range(2):
+                copy(
+                    engs[g],
+                    g32[:, 512 * g : 512 * (g + 1)].rearrange("p (w u) -> p w u", u=2),
+                    banks[g][:].rearrange("p (u w) -> p w u", u=2),
+                )
+            at_grp[(s, gu)] = grp
+
+        def quant_a(s, gu):
+            c = keep.tile([P, 512], U32, name="at_codes%d_%d" % (s, gu), align_bytes=64)
+            sc = keep.tile([P, 512], U8, name="at_scales%d_%d" % (s, gu), align_bytes=64)
+            nc.vector.quantize_mx(out=c[:].bitcast(FP8X4), scales=sc[:], in_=at_grp[(s, gu)][:])
+            at_codes[(s, gu)] = c
+            at_scales[(s, gu)] = sc
+
+        state = {"later": []}
+
+        def defer(n, fn):
+            state["later"] = state["later"] + [[n, fn]]
+
+        def tick():
+            keep_l = []
+            for n, fn in state["later"]:
+                if n <= 1:
+                    fn()
+                else:
+                    keep_l.append([n - 1, fn])
+            state["later"] = keep_l
+
+        hh = {}
+        h_codes = {}
+        h_scales = {}
+
+        def mx_bank(nt, rhs_of):
+            gu, e = nt // 2, nt % 2
+            bank = psum.tile([P, 512], F32, name="bank", tag="bank")
+            for s in range(S):
+                for g in range(2):
+                    cols = slice(256 * g + 128 * e, 256 * g + 128 * (e + 1))
+                    rc, rs = rhs_of(s, g)
+                    nc.tensor.matmul_mx(
+                        out=bank[:, D * s : D * (s + 1)],
+                        lhsT=at_codes[(s, gu)][:, cols].bitcast(FP8X4),
+                        lhsT_scale=at_scales[(s, gu)][:, cols],
+                        rhs=rc.bitcast(FP8X4),
+                        rhs_scale=rs,
+                        start=(g == 0),
+                        stop=(g == 1),
+                    )
+            return bank
+
+        def quant_h(b, g, grp):
+            c = hc_pool.tile([P, 512], U32, name="h_codes", align_bytes=64)
+            sc = hc_pool.tile([P, 512], U8, name="h_scales", align_bytes=64)
+            nc.vector.quantize_mx(out=c[:].bitcast(FP8X4), scales=sc[:], in_=grp[:].rearrange("p s c t -> p (s c t)"))
+            h_codes[(b, g)] = c
+            h_scales[(b, g)] = sc
+
+        def hop1_mm(b, nt):
+            return mx_bank(nt, lambda s, gk: (x_codes[b][:, D * gk : D * (gk + 1)], x_scales[b][:, D * gk : D * (gk + 1)]))
+
+        def hop1_add(b, nt, bank):
+            g, t = nt // 4, nt % 4
+            if t == 0:
+                hh[(b, g)] = hh_pool.tile([P, 4, 2, D, S], F32, name="hh", tag="hh")
+            tl = hh[(b, g)]
+            nc.vector.scalar_tensor_tensor(
+                out=tl[:, t, 0, :, :],
+                in0=x_raw[b][:, nt, :].unsqueeze(2).to_broadcast([P, D, S]),
+                scalar=gain[:, 0:1],
+                in1=bank[:].rearrange("p (s c) -> p c s", s=S),
+                op0=MULT,
+                op1=ADD,
+            )
+            tick()
+            if t == 3 and b > 0:
+                grp = regroup_h(b, g, R_ENG[2 * b + g])
+                defer(DEFER_H, lambda: quant_h(b, g, grp))
+
+        def regroup_h(b, g, engs):
+            grp = hg_pool.tile([P, S, D, 4], BF16, name="h_grp", align_bytes=64)
+            for s in range(S):
+                copy(engs[s], grp[:, s, :, :], hh[(b, g)][:, :, 0, :, s].rearrange("p t c -> p c t"))
+            return grp
+
+        def hop1_unit(b, gu):
+            banks = [hop1_mm(b, 2 * gu + e) for e in range(2)]
+            for e in range(2):
+                hop1_add(b, 2 * gu + e, banks[e])
+
+        def hop2_unit(b, gu, ilv, split):
+            banks = []
+            for e in range(2):
+                banks.append(
+                    mx_bank(
+                        2 * gu + e,
+                        lambda s, gk: (
+                            h_codes[(b, gk)][:, D * s : D * (s + 1)],
+                            h_scales[(b, gk)][:, D * s : D * (s + 1)],
+                        ),
+                    )
+                )
+            o = o_pool.tile([P, 2, 4 * D], F32, name="o")
+            tl = hh[(b, gu // 2)]
+            for e in range(2):
+                t = (2 * gu + e) % 4
+                nc.vector.scalar_tensor_tensor(
+                    out=tl[:, t, 1, :, :],
+                    in0=tl[:, t, 0, :, :],
+                    scalar=gain[:, 0:1],
+                    in1=banks[e][:].rearrange("p (s c) -> p c s", s=S),
+                    op0=MULT,
+                    op1=ADD,
+                )
+                tick()
+            for e in range(2):
+                t = (2 * gu + e) % 4
+                copy(
+                    ilv[e],
+                    o[:, e, :].rearrange("p (f j) -> p f j", j=2),
+                    tl[:, t, :, :, :].rearrange("p j c s -> p (c s) j"),
+                )
+                if split:
+                    nc.sync.dma_start(
+                        out=out[b, 512 * (gu // 2) : 512 * (gu // 2 + 1)].rearrange("(p h e) l f -> h p e (l f)", h=2, e=2)[gu % 2][:, e, :],
+                        in_=o[:, e, :],
+                    )
+            if not split:
+                nc.sync.dma_start(
+                    out=out[b, 512 * (gu // 2) : 512 * (gu // 2 + 1)].rearrange("(p h e) l f -> h p (e l f)", h=2, e=2)[gu % 2],
+                    in_=o[:].rearrange("p e f -> p (e f)"),
+                )
+
+        for b in range(X_FIRST):
+            regroup_x(b)
+            quant_x(b)
+        bank_of = {}
+
+        def mm(nts):
+            for nt in nts:
+                bank_of[nt] = hop1_mm(0, nt)
+
+        def add(nts):
+            for nt in nts:
+                hop1_add(0, nt, bank_of[nt])
+
+        for gu in range(2):
+            for s in range(S):
+                transpose_a(s, gu, E_ENG[2 * gu + s])
+                quant_a(s, gu)
+        mm([0, 1])
+        transpose_a(0, 2, E_ENG[4])
+        transpose_a(1, 2, E_ENG[5])
+        add([0, 1])
+        quant_a(0, 2)
+        quant_a(1, 2)
+        mm([2])
+        transpose_a(0, 3, E_ENG[6])
+        transpose_a(1, 3, E_ENG[7])
+        if X_FIRST < 2:
+            regroup_x(1)
+        add([2])
+        mm([3, 4, 5])
+        add([3])
+        grp00 = regroup_h(0, 0, R_ENG[0])
+        quant_a(0, 3)
+        add([4])
+        quant_a(1, 3)
+        add([5])
+        mm([6, 7])
+        add([6, 7])
+        grp01 = regroup_h(0, 1, R_ENG[1])
+        quant_h(0, 0, grp00)
+        if X_FIRST < 2:
+            quant_x(1)
+        quant_h(0, 1, grp01)
+        if X_FIRST < 3 and XR2_AT < 0:
+            regroup_x(2)
+
+        ones = [(b, gu) for b in range(1, B) for gu in range(4)]
+        twos = [(b, gu) for b in range(B) for gu in range(4)]
+        for b, gu in ones[:PRE]:
+            hop1_unit(b, gu)
+        ones = ones[PRE:]
+        for i, (b, gu) in enumerate(twos):
+            hop2_unit(b, gu, ILV[i], i >= len(twos) - SPLIT_STORES)
+            if i == XR2_AT and X_FIRST < 3:
+                regroup_x(2)
+            if i == XR3_AT and X_FIRST < 4:
+                regroup_x(3)
+            if i == XQ2_AT and X_FIRST < 3:
+                quant_x(2)
+            if i == XQ3_AT and X_FIRST < 4:
+                quant_x(3)
+            for b1, gu1 in ones[: RATES[i]]:
+                hop1_unit(b1, gu1)
+            ones = ones[RATES[i] :]

@@ -17,27 +17,7 @@ D = 256
 S = 2
 NT = 8
 FLOPS = 4 * 2 * 1024 * 1024 * 1024
-
 MANUAL = False
-DEFER_H = 2
-PRE = 1
-X_ENG = ["v", "s", "s", "s"]
-R_ENG = ["ss", "sg", "gs", "sg", "gs", "gg", "gs", "vs"]
-ILV = ["sg", "gs", "sg", "sg", "sv", "gs", "ss", "ss", "sg", "sg", "ss", "sv", "sv", "gs", "sv", "sg"]
-E_ENG = ["vv", "ss", "vs", "ss", "sv", "ss", "ss", "sv"]
-G_SPLIT = 2
-EPS_MM = True
-X_FIRST = 1
-XG_BUFS = 2
-SPLIT_STORES = 0
-E_LAST = ["s", "s"]
-XR2_AT = 0
-XR3_AT = 4
-XQ2_AT = 0
-XQ3_AT = 4
-RATES = [1, 1, 1, 3, 0, 1, 0, 0, 0, 1, 3, 0, 0, 1, 0, 0]
-HH_BUFS = 6
-O_BUFS = 4
 
 
 def tile_ginconvfft_pa_t_kernel(tc, x, support, eps, out):
@@ -45,11 +25,11 @@ def tile_ginconvfft_pa_t_kernel(tc, x, support, eps, out):
     with ExitStack() as ctx:
         keep = ctx.enter_context(tc.tile_pool(name="keep", bufs=1))
         atg_pool = ctx.enter_context(tc.tile_pool(name="atg", bufs=4))
-        xg_pool = ctx.enter_context(tc.tile_pool(name="xg", bufs=XG_BUFS))
-        hh_pool = ctx.enter_context(tc.tile_pool(name="hh", bufs=HH_BUFS))
+        xg_pool = ctx.enter_context(tc.tile_pool(name="xg", bufs=2))
+        hh_pool = ctx.enter_context(tc.tile_pool(name="hh", bufs=6))
         hg_pool = ctx.enter_context(tc.tile_pool(name="hg", bufs=3))
         hc_pool = ctx.enter_context(tc.tile_pool(name="hc", bufs=6))
-        o_pool = ctx.enter_context(tc.tile_pool(name="o", bufs=O_BUFS))
+        o_pool = ctx.enter_context(tc.tile_pool(name="o", bufs=4))
         psum = ctx.enter_context(tc.psum_pool(name="psum", bufs=8))
         if MANUAL:
             ctx.enter_context(tc.manual_schedule())
@@ -60,8 +40,8 @@ def tile_ginconvfft_pa_t_kernel(tc, x, support, eps, out):
             elif eng == "s":
                 nc.scalar.copy(out=dst, in_=src)
             else:
-                n = dst.shape[1] // G_SPLIT
-                for i in range(G_SPLIT):
+                n = dst.shape[1] // 2
+                for i in range(2):
                     nc.gpsimd.tensor_scalar(
                         out=dst[:, i * n : (i + 1) * n],
                         in0=src[:, i * n : (i + 1) * n],
@@ -73,20 +53,10 @@ def tile_ginconvfft_pa_t_kernel(tc, x, support, eps, out):
 
         ident = keep.tile([P, P], F32, name="ident")
         make_identity(nc, ident[:])
-        gain = keep.tile([P, 1], F32, name="gain")
-        if EPS_MM:
-            eps_row = keep.tile([P, 32], BF16, name="eps_row")
-            nc.vector.memset(eps_row[:], 0.0)
-            ones = keep.tile([P, P], BF16, name="ones")
-            nc.vector.memset(ones[:], 1.0)
-            nc.scalar.dma_start(out=eps_row[0:1, 0:1], in_=eps.rearrange("(o n) -> o n", o=1))
-            eps_bank = psum.tile([P, 512], F32, name="bank", tag="bank")
-            nc.tensor.matmul(out=eps_bank[:, 0:32], lhsT=ones[:], rhs=eps_row[:], start=True, stop=True)
-            nc.vector.tensor_scalar_add(out=gain[:], in0=eps_bank[:, 0:1], scalar1=1.0)
-        else:
-            eps_sb = keep.tile([P, 1], BF16, name="eps_sb")
-            nc.scalar.dma_start(out=eps_sb[:], in_=eps.partition_broadcast(P))
-            nc.vector.tensor_scalar_add(out=gain[:], in0=eps_sb[:], scalar1=1.0)
+        eps_row = keep.tile([P, 32], BF16, name="eps_row")
+        nc.vector.memset(eps_row[:], 0.0)
+        ones = keep.tile([P, P], BF16, name="ones")
+        nc.vector.memset(ones[:], 1.0)
 
         x_raw = {}
         a_raw = {}
@@ -107,22 +77,22 @@ def tile_ginconvfft_pa_t_kernel(tc, x, support, eps, out):
                 in_=support[s, 512 * (gu // 2) : 512 * (gu // 2 + 1), :].rearrange("(p h e) m -> h p (e m)", h=2, e=2)[gu % 2],
             )
 
-        for b in range(X_FIRST):
-            load_x(b)
+        load_x(0)
+        nc.sync.dma_start(out=eps_row[0:1, 0:1], in_=eps.rearrange("(o n) -> o n", o=1))
         for gu in range(4):
             for s in range(S):
                 load_a(s, gu)
-        for b in range(X_FIRST, B):
+        for b in range(1, B):
             load_x(b)
 
         x_grp = {}
         x_codes = {}
         x_scales = {}
 
-        def regroup_x(b):
+        def regroup_x(b, engs):
             t = xg_pool.tile([P, 2, D, 4], BF16, name="x_grp", align_bytes=64)
             for g in range(2):
-                copy(X_ENG[b], t[:, g, :, :], x_raw[b][:, 4 * g : 4 * (g + 1), :].rearrange("p t d -> p d t"))
+                copy(engs[g], t[:, g, :, :], x_raw[b][:, 4 * g : 4 * (g + 1), :].rearrange("p t d -> p d t"))
             x_grp[b] = t
 
         def quant_x(b):
@@ -169,23 +139,10 @@ def tile_ginconvfft_pa_t_kernel(tc, x, support, eps, out):
             at_codes[(s, gu)] = c
             at_scales[(s, gu)] = sc
 
-        state = {"later": []}
-
-        def defer(n, fn):
-            state["later"] = state["later"] + [[n, fn]]
-
-        def tick():
-            keep_l = []
-            for n, fn in state["later"]:
-                if n <= 1:
-                    fn()
-                else:
-                    keep_l.append([n - 1, fn])
-            state["later"] = keep_l
-
         hh = {}
         h_codes = {}
         h_scales = {}
+        bank1 = {}
 
         def mx_bank(nt, rhs_of):
             gu, e = nt // 2, nt % 2
@@ -205,149 +162,130 @@ def tile_ginconvfft_pa_t_kernel(tc, x, support, eps, out):
                     )
             return bank
 
-        def quant_h(b, g, grp):
-            c = hc_pool.tile([P, 512], U32, name="h_codes", align_bytes=64)
-            sc = hc_pool.tile([P, 512], U8, name="h_scales", align_bytes=64)
-            nc.vector.quantize_mx(out=c[:].bitcast(FP8X4), scales=sc[:], in_=grp[:].rearrange("p s c t -> p (s c t)"))
-            h_codes[(b, g)] = c
-            h_scales[(b, g)] = sc
+        def mm1(b, gu):
+            for nt in (2 * gu, 2 * gu + 1):
+                bank1[(b, nt)] = mx_bank(
+                    nt, lambda s, gk: (x_codes[b][:, D * gk : D * (gk + 1)], x_scales[b][:, D * gk : D * (gk + 1)])
+                )
 
-        def hop1_mm(b, nt):
-            return mx_bank(nt, lambda s, gk: (x_codes[b][:, D * gk : D * (gk + 1)], x_scales[b][:, D * gk : D * (gk + 1)]))
-
-        def hop1_add(b, nt, bank):
-            g, t = nt // 4, nt % 4
-            if t == 0:
+        def add1(b, gu):
+            g = gu // 2
+            if gu % 2 == 0:
                 hh[(b, g)] = hh_pool.tile([P, 4, 2, D, S], F32, name="hh", tag="hh")
             tl = hh[(b, g)]
-            nc.vector.scalar_tensor_tensor(
-                out=tl[:, t, 0, :, :],
-                in0=x_raw[b][:, nt, :].unsqueeze(2).to_broadcast([P, D, S]),
-                scalar=gain[:, 0:1],
-                in1=bank[:].rearrange("p (s c) -> p c s", s=S),
-                op0=MULT,
-                op1=ADD,
-            )
-            tick()
-            if t == 3 and b > 0:
-                grp = regroup_h(b, g, R_ENG[2 * b + g])
-                defer(DEFER_H, lambda: quant_h(b, g, grp))
-
-        def regroup_h(b, g, engs):
-            grp = hg_pool.tile([P, S, D, 4], BF16, name="h_grp", align_bytes=64)
-            for s in range(S):
-                copy(engs[s], grp[:, s, :, :], hh[(b, g)][:, :, 0, :, s].rearrange("p t c -> p c t"))
-            return grp
-
-        def hop1_unit(b, gu):
-            banks = [hop1_mm(b, 2 * gu + e) for e in range(2)]
-            for e in range(2):
-                hop1_add(b, 2 * gu + e, banks[e])
-
-        def hop2_unit(b, gu, ilv, split):
-            banks = []
-            for e in range(2):
-                banks.append(
-                    mx_bank(
-                        2 * gu + e,
-                        lambda s, gk: (
-                            h_codes[(b, gk)][:, D * s : D * (s + 1)],
-                            h_scales[(b, gk)][:, D * s : D * (s + 1)],
-                        ),
-                    )
-                )
-            o = o_pool.tile([P, 2, 4 * D], F32, name="o")
-            tl = hh[(b, gu // 2)]
-            for e in range(2):
-                t = (2 * gu + e) % 4
+            for nt in (2 * gu, 2 * gu + 1):
                 nc.vector.scalar_tensor_tensor(
-                    out=tl[:, t, 1, :, :],
-                    in0=tl[:, t, 0, :, :],
+                    out=tl[:, nt % 4, 0, :, :],
+                    in0=x_raw[b][:, nt, :].unsqueeze(2).to_broadcast([P, D, S]),
                     scalar=gain[:, 0:1],
-                    in1=banks[e][:].rearrange("p (s c) -> p c s", s=S),
+                    in1=bank1[(b, nt)][:].rearrange("p (s c) -> p c s", s=S),
                     op0=MULT,
                     op1=ADD,
                 )
-                tick()
-            for e in range(2):
-                t = (2 * gu + e) % 4
-                copy(
-                    ilv[e],
-                    o[:, e, :].rearrange("p (f j) -> p f j", j=2),
-                    tl[:, t, :, :, :].rearrange("p j c s -> p (c s) j"),
-                )
-                if split:
-                    nc.sync.dma_start(
-                        out=out[b, 512 * (gu // 2) : 512 * (gu // 2 + 1)].rearrange("(p h e) l f -> h p e (l f)", h=2, e=2)[gu % 2][:, e, :],
-                        in_=o[:, e, :],
-                    )
-            if not split:
-                nc.sync.dma_start(
-                    out=out[b, 512 * (gu // 2) : 512 * (gu // 2 + 1)].rearrange("(p h e) l f -> h p (e l f)", h=2, e=2)[gu % 2],
-                    in_=o[:].rearrange("p e f -> p (e f)"),
-                )
 
-        for b in range(X_FIRST):
-            regroup_x(b)
-            quant_x(b)
-        bank_of = {}
+        h_grp = {}
 
-        def mm(nts):
-            for nt in nts:
-                bank_of[nt] = hop1_mm(0, nt)
-
-        def add(nts):
-            for nt in nts:
-                hop1_add(0, nt, bank_of[nt])
-
-        for gu in range(2):
+        def regroup_h(b, g):
+            grp = hg_pool.tile([P, S, D, 4], BF16, name="h_grp", align_bytes=64)
             for s in range(S):
-                transpose_a(s, gu, E_ENG[2 * gu + s])
-                quant_a(s, gu)
-        mm([0, 1])
-        transpose_a(0, 2, E_ENG[4])
-        transpose_a(1, 2, E_ENG[5])
-        add([0, 1])
-        quant_a(0, 2)
-        quant_a(1, 2)
-        mm([2])
-        transpose_a(0, 3, E_ENG[6])
-        transpose_a(1, 3, E_ENG[7])
-        if X_FIRST < 2:
-            regroup_x(1)
-        add([2])
-        mm([3, 4, 5])
-        add([3])
-        grp00 = regroup_h(0, 0, R_ENG[0])
-        quant_a(0, 3)
-        add([4])
-        quant_a(1, 3)
-        add([5])
-        mm([6, 7])
-        add([6, 7])
-        grp01 = regroup_h(0, 1, R_ENG[1])
-        quant_h(0, 0, grp00)
-        if X_FIRST < 2:
-            quant_x(1)
-        quant_h(0, 1, grp01)
-        if X_FIRST < 3 and XR2_AT < 0:
-            regroup_x(2)
+                copy("sg"[s], grp[:, s, :, :], hh[(b, g)][:, :, 0, :, s].rearrange("p t c -> p c t"))
+            h_grp[(b, g)] = grp
 
-        ones = [(b, gu) for b in range(1, B) for gu in range(4)]
-        twos = [(b, gu) for b in range(B) for gu in range(4)]
-        for b, gu in ones[:PRE]:
-            hop1_unit(b, gu)
-        ones = ones[PRE:]
-        for i, (b, gu) in enumerate(twos):
-            hop2_unit(b, gu, ILV[i], i >= len(twos) - SPLIT_STORES)
-            if i == XR2_AT and X_FIRST < 3:
-                regroup_x(2)
-            if i == XR3_AT and X_FIRST < 4:
-                regroup_x(3)
-            if i == XQ2_AT and X_FIRST < 3:
-                quant_x(2)
-            if i == XQ3_AT and X_FIRST < 4:
-                quant_x(3)
-            for b1, gu1 in ones[: RATES[i]]:
-                hop1_unit(b1, gu1)
-            ones = ones[RATES[i] :]
+        def quant_h(b, g):
+            c = hc_pool.tile([P, 512], U32, name="h_codes", align_bytes=64)
+            sc = hc_pool.tile([P, 512], U8, name="h_scales", align_bytes=64)
+            nc.vector.quantize_mx(
+                out=c[:].bitcast(FP8X4), scales=sc[:], in_=h_grp[(b, g)][:].rearrange("p s c t -> p (s c t)")
+            )
+            h_codes[(b, g)] = c
+            h_scales[(b, g)] = sc
+
+        bank2 = {}
+
+        def mm2(b, gu):
+            for nt in (2 * gu, 2 * gu + 1):
+                bank2[(b, nt)] = mx_bank(
+                    nt, lambda s, gk: (h_codes[(b, gk)][:, D * s : D * (s + 1)], h_scales[(b, gk)][:, D * s : D * (s + 1)])
+                )
+
+        def add2(b, gu):
+            tl = hh[(b, gu // 2)]
+            for nt in (2 * gu, 2 * gu + 1):
+                nc.vector.scalar_tensor_tensor(
+                    out=tl[:, nt % 4, 1, :, :],
+                    in0=tl[:, nt % 4, 0, :, :],
+                    scalar=gain[:, 0:1],
+                    in1=bank2[(b, nt)][:].rearrange("p (s c) -> p c s", s=S),
+                    op0=MULT,
+                    op1=ADD,
+                )
+
+        def store(b, gu, engs):
+            tl = hh[(b, gu // 2)]
+            o = o_pool.tile([P, 2, 4 * D], F32, name="o")
+            for e in range(2):
+                copy(
+                    engs[e],
+                    o[:, e, :].rearrange("p (f j) -> p f j", j=2),
+                    tl[:, (2 * gu + e) % 4, :, :, :].rearrange("p j c s -> p (c s) j"),
+                )
+            nc.sync.dma_start(
+                out=out[b, 512 * (gu // 2) : 512 * (gu // 2 + 1)].rearrange("(p h e) l f -> h p (e l f)", h=2, e=2)[gu % 2],
+                in_=o[:].rearrange("p e f -> p (e f)"),
+            )
+
+        regroup_x(0, "vv")
+        transpose_a(0, 0, "ss")
+        transpose_a(1, 0, "ss")
+        quant_x(0)
+        eps_bank = psum.tile([P, 512], F32, name="bank", tag="bank")
+        nc.tensor.matmul(out=eps_bank[:, 0:32], lhsT=ones[:], rhs=eps_row[:], start=True, stop=True)
+        gain = keep.tile([P, 1], F32, name="gain")
+        nc.vector.tensor_scalar_add(out=gain[:], in0=eps_bank[:, 0:1], scalar1=1.0)
+        quant_a(0, 0)
+        quant_a(1, 0)
+        for gu in range(1, 4):
+            for s in range(S):
+                transpose_a(s, gu, "ss")
+            mm1(0, gu - 1)
+            for s in range(S):
+                quant_a(s, gu)
+            add1(0, gu - 1)
+        regroup_h(0, 0)
+        mm1(0, 3)
+        add1(0, 3)
+        regroup_x(1, "vv")
+        regroup_h(0, 1)
+        quant_h(0, 0)
+        quant_x(1)
+        mm1(1, 0)
+        mm1(1, 1)
+        add1(1, 0)
+        quant_h(0, 1)
+        add1(1, 1)
+
+        regroup_h(1, 0)
+        regroup_x(2, "ss")
+
+        hop1_units = [(b, gu) for b in range(1, B) for gu in range(4)][2:]
+        hop2_units = [(b, gu) for b in range(B) for gu in range(4)]
+        ready = [(1, 0)]
+        for i, (b, gu) in enumerate(hop2_units):
+            unit = hop1_units[i] if i < len(hop1_units) else None
+            mm2(b, gu)
+            if unit:
+                mm1(unit[0], unit[1])
+            add2(b, gu)
+            for half in ready:
+                quant_h(half[0], half[1])
+            ready = []
+            store(b, gu, "sg")
+            if unit:
+                add1(unit[0], unit[1])
+                if unit[1] % 2 == 1:
+                    regroup_h(unit[0], unit[1] // 2)
+                    ready = [(unit[0], unit[1] // 2)]
+            if i in (0, 4):
+                quant_x(2 + i // 4)
+            if i == 2:
+                regroup_x(3, "ss")

@@ -17,7 +17,8 @@ D = 256
 S = 2
 NT = 8
 FLOPS = 4 * 2 * 1024 * 1024 * 1024
-MANUAL = False
+
+CHUNKS = [(b, c, 128) for b in range(4) for c in (0, 128)]
 
 
 def tile_ginconvfft_pa_t_kernel(tc, x, support, eps, out):
@@ -26,13 +27,12 @@ def tile_ginconvfft_pa_t_kernel(tc, x, support, eps, out):
         keep = ctx.enter_context(tc.tile_pool(name="keep", bufs=1))
         atg_pool = ctx.enter_context(tc.tile_pool(name="atg", bufs=4))
         xg_pool = ctx.enter_context(tc.tile_pool(name="xg", bufs=2))
-        hh_pool = ctx.enter_context(tc.tile_pool(name="hh", bufs=6))
-        hg_pool = ctx.enter_context(tc.tile_pool(name="hg", bufs=3))
+        hh_pool = ctx.enter_context(tc.tile_pool(name="hh", bufs=10))
+        hg_pool = ctx.enter_context(tc.tile_pool(name="hg", bufs=4))
         hc_pool = ctx.enter_context(tc.tile_pool(name="hc", bufs=6))
-        o_pool = ctx.enter_context(tc.tile_pool(name="o", bufs=4))
+        o_pool = ctx.enter_context(tc.tile_pool(name="o", bufs=12))
         psum = ctx.enter_context(tc.psum_pool(name="psum", bufs=8))
-        if MANUAL:
-            ctx.enter_context(tc.manual_schedule())
+        ctx.enter_context(tc.manual_schedule())
 
         def copy(eng, dst, src):
             if eng == "v":
@@ -40,23 +40,14 @@ def tile_ginconvfft_pa_t_kernel(tc, x, support, eps, out):
             elif eng == "s":
                 nc.scalar.copy(out=dst, in_=src)
             else:
-                n = dst.shape[1] // 2
-                for i in range(2):
-                    nc.gpsimd.tensor_scalar(
-                        out=dst[:, i * n : (i + 1) * n],
-                        in0=src[:, i * n : (i + 1) * n],
-                        scalar1=1.0,
-                        scalar2=0.0,
-                        op0=MULT,
-                        op1=ADD,
-                    )
+                nc.gpsimd.tensor_scalar(out=dst, in0=src, scalar1=1.0, scalar2=0.0, op0=MULT, op1=ADD)
 
-        ident = keep.tile([P, P], F32, name="ident")
-        make_identity(nc, ident[:])
         eps_row = keep.tile([P, 32], BF16, name="eps_row")
         nc.vector.memset(eps_row[:], 0.0)
         ones = keep.tile([P, P], BF16, name="ones")
         nc.vector.memset(ones[:], 1.0)
+        ident = keep.tile([P, P], F32, name="ident")
+        make_identity(nc, ident[:])
 
         x_raw = {}
         a_raw = {}
@@ -70,10 +61,10 @@ def tile_ginconvfft_pa_t_kernel(tc, x, support, eps, out):
             x_raw[b] = t
 
         def load_a(s, gu):
-            if (gu // 2) not in a_raw:
-                a_raw[gu // 2] = hh_pool.tile([P, 4, 2048], BF16, name="a_raw", tag="hh")
+            if s == 0:
+                a_raw[gu] = hh_pool.tile([P, S, 2048], BF16, name="a_raw", tag="hh")
             nc.sync.dma_start(
-                out=a_raw[gu // 2][:, 2 * (gu % 2) + s, :],
+                out=a_raw[gu][:, s, :],
                 in_=support[s, 512 * (gu // 2) : 512 * (gu // 2 + 1), :].rearrange("(p h e) m -> h p (e m)", h=2, e=2)[gu % 2],
             )
 
@@ -108,184 +99,196 @@ def tile_ginconvfft_pa_t_kernel(tc, x, support, eps, out):
         at_codes = {}
         at_scales = {}
 
-        def transpose_a(s, gu, engs):
-            a32 = a_raw[gu // 2][:, 2 * (gu % 2) + s, :].bitcast(F32)
-            grp = atg_pool.tile([P, 2048], BF16, name="at_grp", align_bytes=64)
-            g32 = grp[:].bitcast(F32)
-            banks = []
-            for g in range(2):
-                bank = psum.tile([P, 512], F32, name="bank", tag="bank")
-                for u in range(2):
-                    for e in range(2):
-                        w0 = 512 * e + 256 * g
-                        nc.tensor.transpose(
-                            out=bank[:, 256 * u + 128 * e : 256 * u + 128 * (e + 1)],
-                            in_=a32[:, w0 + u : w0 + 256 : 2],
-                            identity=ident[:],
-                        )
-                banks.append(bank)
-            for g in range(2):
-                copy(
-                    engs[g],
-                    g32[:, 512 * g : 512 * (g + 1)].rearrange("p (w u) -> p w u", u=2),
-                    banks[g][:].rearrange("p (u w) -> p w u", u=2),
-                )
-            at_grp[(s, gu)] = grp
+        def transpose_a(gu, engs):
+            for s in range(S):
+                a32 = a_raw[gu][:, s, :].bitcast(F32)
+                grp = atg_pool.tile([P, 2048], BF16, name="at_grp", align_bytes=64)
+                g32 = grp[:].bitcast(F32)
+                for g in range(2):
+                    bank = psum.tile([P, 512], F32, name="bank", tag="bank")
+                    for u in range(2):
+                        for e in range(2):
+                            w0 = 512 * e + 256 * g
+                            nc.tensor.transpose(
+                                out=bank[:, 256 * u + 128 * e : 256 * u + 128 * (e + 1)],
+                                in_=a32[:, w0 + u : w0 + 256 : 2],
+                                identity=ident[:],
+                            )
+                    copy(
+                        engs[2 * s + g],
+                        g32[:, 512 * g : 512 * (g + 1)].rearrange("p (w u) -> p w u", u=2),
+                        bank[:].rearrange("p (u w) -> p w u", u=2),
+                    )
+                at_grp[(s, gu)] = grp
 
-        def quant_a(s, gu):
-            c = keep.tile([P, 512], U32, name="at_codes%d_%d" % (s, gu), align_bytes=64)
-            sc = keep.tile([P, 512], U8, name="at_scales%d_%d" % (s, gu), align_bytes=64)
-            nc.vector.quantize_mx(out=c[:].bitcast(FP8X4), scales=sc[:], in_=at_grp[(s, gu)][:])
-            at_codes[(s, gu)] = c
-            at_scales[(s, gu)] = sc
+        def quant_a(gu):
+            for s in range(S):
+                c = keep.tile([P, 512], U32, name="at_codes%d_%d" % (s, gu), align_bytes=64)
+                sc = keep.tile([P, 512], U8, name="at_scales%d_%d" % (s, gu), align_bytes=64)
+                nc.vector.quantize_mx(out=c[:].bitcast(FP8X4), scales=sc[:], in_=at_grp[(s, gu)][:])
+                at_codes[(s, gu)] = c
+                at_scales[(s, gu)] = sc
 
         hh = {}
+        h_grp = {}
         h_codes = {}
         h_scales = {}
-        bank1 = {}
+        banks = {}
 
-        def mx_bank(nt, rhs_of):
-            gu, e = nt // 2, nt % 2
+        def shape_of(ch):
+            b, c0, w = CHUNKS[ch]
+            return b, c0, w, 256 // w
+
+        def mx_bank(ch, k, rhs_of):
+            b, c0, w, n_t = shape_of(ch)
             bank = psum.tile([P, 512], F32, name="bank", tag="bank")
-            for s in range(S):
-                for g in range(2):
-                    cols = slice(256 * g + 128 * e, 256 * g + 128 * (e + 1))
-                    rc, rs = rhs_of(s, g)
-                    nc.tensor.matmul_mx(
-                        out=bank[:, D * s : D * (s + 1)],
-                        lhsT=at_codes[(s, gu)][:, cols].bitcast(FP8X4),
-                        lhsT_scale=at_scales[(s, gu)][:, cols],
-                        rhs=rc.bitcast(FP8X4),
-                        rhs_scale=rs,
-                        start=(g == 0),
-                        stop=(g == 1),
-                    )
+            for i in range(n_t):
+                nt = n_t * k + i
+                gu, e = nt // 2, nt % 2
+                for s in range(S):
+                    for g in range(2):
+                        cols = slice(256 * g + 128 * e, 256 * g + 128 * (e + 1))
+                        rc, rs = rhs_of(s, g)
+                        nc.tensor.matmul_mx(
+                            out=bank[:, w * (n_t * s + i) : w * (n_t * s + i + 1)],
+                            lhsT=at_codes[(s, gu)][:, cols].bitcast(FP8X4),
+                            lhsT_scale=at_scales[(s, gu)][:, cols],
+                            rhs=rc.bitcast(FP8X4),
+                            rhs_scale=rs,
+                            start=(g == 0),
+                            stop=(g == 1),
+                        )
             return bank
 
-        def mm1(b, gu):
-            for nt in (2 * gu, 2 * gu + 1):
-                bank1[(b, nt)] = mx_bank(
-                    nt, lambda s, gk: (x_codes[b][:, D * gk : D * (gk + 1)], x_scales[b][:, D * gk : D * (gk + 1)])
-                )
+        def mm1(ch, k):
+            b, c0, w, n_t = shape_of(ch)
 
-        def add1(b, gu):
-            g = gu // 2
-            if gu % 2 == 0:
-                hh[(b, g)] = hh_pool.tile([P, 4, 2, D, S], F32, name="hh", tag="hh")
-            tl = hh[(b, g)]
-            for nt in (2 * gu, 2 * gu + 1):
+            def rhs_of(s, g):
+                cols = slice(D * g + c0, D * g + c0 + w)
+                return x_codes[b][:, cols], x_scales[b][:, cols]
+
+            banks[(1, ch, k)] = mx_bank(ch, k, rhs_of)
+
+        def mm2(ch, k):
+            b, c0, w, n_t = shape_of(ch)
+
+            def rhs_of(s, g):
+                cols = slice(w * s, w * (s + 1))
+                return h_codes[(ch, g)][:, cols], h_scales[(ch, g)][:, cols]
+
+            banks[(2, ch, k)] = mx_bank(ch, k, rhs_of)
+
+        def add1(ch, k):
+            b, c0, w, n_t = shape_of(ch)
+            t0 = n_t * k % 4
+            if t0 == 0:
+                hh[(ch, n_t * k // 4)] = hh_pool.tile([P, 4, 2, w, S], F32, name="hh", tag="hh")
+            for i in range(n_t):
                 nc.vector.scalar_tensor_tensor(
-                    out=tl[:, nt % 4, 0, :, :],
-                    in0=x_raw[b][:, nt, :].unsqueeze(2).to_broadcast([P, D, S]),
+                    out=hh[(ch, n_t * k // 4)][:, t0 + i, 0, :, :],
+                    in0=x_raw[b][:, n_t * k + i, c0 : c0 + w].unsqueeze(2).to_broadcast([P, w, S]),
                     scalar=gain[:, 0:1],
-                    in1=bank1[(b, nt)][:].rearrange("p (s c) -> p c s", s=S),
+                    in1=banks[(1, ch, k)][:].rearrange("p (s i c) -> p i c s", s=S, c=w)[:, i, :, :],
                     op0=MULT,
                     op1=ADD,
                 )
 
-        h_grp = {}
+        def add2(ch, k):
+            b, c0, w, n_t = shape_of(ch)
+            t0 = n_t * k % 4
+            tl = hh[(ch, n_t * k // 4)]
+            nc.vector.scalar_tensor_tensor(
+                out=tl[:, t0 : t0 + n_t, 1, :, :],
+                in0=tl[:, t0 : t0 + n_t, 0, :, :],
+                scalar=gain[:, 0:1],
+                in1=banks[(2, ch, k)][:].rearrange("p (s i c) -> p i c s", s=S, c=w),
+                op0=MULT,
+                op1=ADD,
+            )
 
-        def regroup_h(b, g):
-            grp = hg_pool.tile([P, S, D, 4], BF16, name="h_grp", align_bytes=64)
+        def regroup_h(ch, g, engs):
+            b, c0, w, n_t = shape_of(ch)
+            grp = hg_pool.tile([P, S, w, 4], BF16, name="h_grp", align_bytes=64, tag="hg%d" % w)
             for s in range(S):
-                copy("sg"[s], grp[:, s, :, :], hh[(b, g)][:, :, 0, :, s].rearrange("p t c -> p c t"))
-            h_grp[(b, g)] = grp
+                copy(engs[s], grp[:, s, :, :], hh[(ch, g)][:, :, 0, :, s].rearrange("p t c -> p c t"))
+            h_grp[(ch, g)] = grp
 
-        def quant_h(b, g):
-            c = hc_pool.tile([P, 512], U32, name="h_codes", align_bytes=64)
-            sc = hc_pool.tile([P, 512], U8, name="h_scales", align_bytes=64)
+        def quant_h(ch, g):
+            b, c0, w, n_t = shape_of(ch)
+            c = hc_pool.tile([P, S * w], U32, name="h_codes", align_bytes=64, tag="hc%d" % w)
+            sc = hc_pool.tile([P, S * w], U8, name="h_scales", align_bytes=64, tag="hs%d" % w)
             nc.vector.quantize_mx(
-                out=c[:].bitcast(FP8X4), scales=sc[:], in_=h_grp[(b, g)][:].rearrange("p s c t -> p (s c t)")
+                out=c[:].bitcast(FP8X4), scales=sc[:], in_=h_grp[(ch, g)][:].rearrange("p s c t -> p (s c t)")
             )
-            h_codes[(b, g)] = c
-            h_scales[(b, g)] = sc
+            h_codes[(ch, g)] = c
+            h_scales[(ch, g)] = sc
 
-        bank2 = {}
-
-        def mm2(b, gu):
-            for nt in (2 * gu, 2 * gu + 1):
-                bank2[(b, nt)] = mx_bank(
-                    nt, lambda s, gk: (h_codes[(b, gk)][:, D * s : D * (s + 1)], h_scales[(b, gk)][:, D * s : D * (s + 1)])
-                )
-
-        def add2(b, gu):
-            tl = hh[(b, gu // 2)]
-            for nt in (2 * gu, 2 * gu + 1):
-                nc.vector.scalar_tensor_tensor(
-                    out=tl[:, nt % 4, 1, :, :],
-                    in0=tl[:, nt % 4, 0, :, :],
-                    scalar=gain[:, 0:1],
-                    in1=bank2[(b, nt)][:].rearrange("p (s c) -> p c s", s=S),
-                    op0=MULT,
-                    op1=ADD,
-                )
-
-        def store(b, gu, engs):
-            tl = hh[(b, gu // 2)]
-            o = o_pool.tile([P, 2, 4 * D], F32, name="o")
-            for e in range(2):
-                copy(
-                    engs[e],
-                    o[:, e, :].rearrange("p (f j) -> p f j", j=2),
-                    tl[:, (2 * gu + e) % 4, :, :, :].rearrange("p j c s -> p (c s) j"),
-                )
-            nc.sync.dma_start(
-                out=out[b, 512 * (gu // 2) : 512 * (gu // 2 + 1)].rearrange("(p h e) l f -> h p (e l f)", h=2, e=2)[gu % 2],
-                in_=o[:].rearrange("p e f -> p (e f)"),
+        def store(ch, k, eng):
+            b, c0, w, n_t = shape_of(ch)
+            g, t0 = n_t * k // 4, n_t * k % 4
+            o = o_pool.tile([P, n_t, 4 * w], F32, name="o")
+            copy(
+                eng,
+                o[:].rearrange("p i (f j) -> p i f j", j=2),
+                hh[(ch, g)][:, t0 : t0 + n_t, :, :, :].rearrange("p i j c s -> p i (c s) j"),
             )
+            dst = out[b, 512 * g : 512 * (g + 1)].rearrange("(p t) l f -> p t (l f)", t=4)
+            nc.sync.dma_start(out=dst[:, t0 : t0 + n_t, 4 * c0 : 4 * (c0 + w)], in_=o[:])
+
+        def hop1(i):
+            add1(i // 4, i % 4)
 
         regroup_x(0, "vv")
-        transpose_a(0, 0, "ss")
-        transpose_a(1, 0, "ss")
         quant_x(0)
+        transpose_a(0, "ssss")
+        transpose_a(1, "ssss")
         eps_bank = psum.tile([P, 512], F32, name="bank", tag="bank")
         nc.tensor.matmul(out=eps_bank[:, 0:32], lhsT=ones[:], rhs=eps_row[:], start=True, stop=True)
         gain = keep.tile([P, 1], F32, name="gain")
+        quant_a(0)
         nc.vector.tensor_scalar_add(out=gain[:], in0=eps_bank[:, 0:1], scalar1=1.0)
-        quant_a(0, 0)
-        quant_a(1, 0)
-        for gu in range(1, 4):
-            for s in range(S):
-                transpose_a(s, gu, "ss")
-            mm1(0, gu - 1)
-            for s in range(S):
-                quant_a(s, gu)
-            add1(0, gu - 1)
-        regroup_h(0, 0)
+        mm1(0, 0)
+        transpose_a(2, "ssss")
+        quant_a(1)
+        hop1(0)
+        mm1(0, 1)
+        transpose_a(3, "ssss")
+        quant_a(2)
+        hop1(1)
+        regroup_h(0, 0, "gg")
+        mm1(0, 2)
+        quant_a(3)
+        hop1(2)
         mm1(0, 3)
-        add1(0, 3)
-        regroup_x(1, "vv")
-        regroup_h(0, 1)
         quant_h(0, 0)
-        quant_x(1)
         mm1(1, 0)
+        hop1(3)
+        regroup_h(0, 1, "sg")
         mm1(1, 1)
-        add1(1, 0)
+        regroup_x(1, "ss")
+        hop1(4)
+        hop1(5)
+        regroup_h(1, 0, "sg")
         quant_h(0, 1)
-        add1(1, 1)
+        mm2(0, 0)
+        mm1(1, 2)
 
-        regroup_h(1, 0)
-        regroup_x(2, "ss")
-
-        hop1_units = [(b, gu) for b in range(1, B) for gu in range(4)][2:]
-        hop2_units = [(b, gu) for b in range(B) for gu in range(4)]
-        ready = [(1, 0)]
-        for i, (b, gu) in enumerate(hop2_units):
-            unit = hop1_units[i] if i < len(hop1_units) else None
-            mm2(b, gu)
-            if unit:
-                mm1(unit[0], unit[1])
-            add2(b, gu)
-            for half in ready:
-                quant_h(half[0], half[1])
-            ready = []
-            store(b, gu, "sg")
-            if unit:
-                add1(unit[0], unit[1])
-                if unit[1] % 2 == 1:
-                    regroup_h(unit[0], unit[1] // 2)
-                    ready = [(unit[0], unit[1] // 2)]
-            if i in (0, 4):
-                quant_x(2 + i // 4)
-            if i == 2:
-                regroup_x(3, "ss")
+        LEAD = 6
+        for i in range(32):
+            j = i + LEAD
+            if i % 2 == 1 and j - 3 < 32:
+                quant_h((j - 3) // 4, (j - 3) // 2 % 2)
+            if i in (1, 8, 16):
+                quant_x(1 + i // 8)
+            if i + 1 < 32:
+                mm2((i + 1) // 4, (i + 1) % 4)
+            if j + 1 < 32:
+                mm1((j + 1) // 4, (j + 1) % 4)
+            if j < 32:
+                hop1(j)
+                if j % 2 == 1:
+                    regroup_h(j // 4, j // 2 % 2, "sg")
+            add2(i // 4, i % 4)
+            store(i // 4, i % 4, ("sg" if j < 32 else "sv")[i % 2])
+            if i in (3, 11):
+                regroup_x(2 + i // 8, "sg")

@@ -18,7 +18,7 @@ S = 2
 NT = 8
 FLOPS = 4 * 2 * 1024 * 1024 * 1024
 
-CHUNKS = [(b, c, 128) for b in range(4) for c in (0, 128)]
+CHUNKS = [(b, 0, 256) for b in range(4)]
 
 
 def tile_ginconvfft_pa_t_kernel(tc, x, support, eps, out):
@@ -27,12 +27,11 @@ def tile_ginconvfft_pa_t_kernel(tc, x, support, eps, out):
         keep = ctx.enter_context(tc.tile_pool(name="keep", bufs=1))
         atg_pool = ctx.enter_context(tc.tile_pool(name="atg", bufs=4))
         xg_pool = ctx.enter_context(tc.tile_pool(name="xg", bufs=2))
-        hh_pool = ctx.enter_context(tc.tile_pool(name="hh", bufs=10))
-        hg_pool = ctx.enter_context(tc.tile_pool(name="hg", bufs=4))
-        hc_pool = ctx.enter_context(tc.tile_pool(name="hc", bufs=6))
-        o_pool = ctx.enter_context(tc.tile_pool(name="o", bufs=12))
+        hh_pool = ctx.enter_context(tc.tile_pool(name="hh", bufs=6))
+        hg_pool = ctx.enter_context(tc.tile_pool(name="hg", bufs=2))
+        hc_pool = ctx.enter_context(tc.tile_pool(name="hc", bufs=4))
+        o_pool = ctx.enter_context(tc.tile_pool(name="o", bufs=5))
         psum = ctx.enter_context(tc.psum_pool(name="psum", bufs=8))
-        ctx.enter_context(tc.manual_schedule())
 
         def copy(eng, dst, src):
             if eng == "v":
@@ -40,7 +39,12 @@ def tile_ginconvfft_pa_t_kernel(tc, x, support, eps, out):
             elif eng == "s":
                 nc.scalar.copy(out=dst, in_=src)
             else:
-                nc.gpsimd.tensor_scalar(out=dst, in0=src, scalar1=1.0, scalar2=0.0, op0=MULT, op1=ADD)
+                axis = 1 if dst.shape[1] > 2 else 2
+                n = dst.shape[axis] // 2
+                for i in range(2):
+                    part = slice(i * n, (i + 1) * n)
+                    d, f = (dst[:, part], src[:, part]) if axis == 1 else (dst[:, :, part], src[:, :, part])
+                    nc.gpsimd.tensor_scalar(out=d, in0=f, scalar1=1.0, scalar2=0.0, op0=MULT, op1=ADD)
 
         eps_row = keep.tile([P, 32], BF16, name="eps_row")
         nc.vector.memset(eps_row[:], 0.0)
@@ -61,20 +65,26 @@ def tile_ginconvfft_pa_t_kernel(tc, x, support, eps, out):
             x_raw[b] = t
 
         def load_a(s, gu):
-            if s == 0:
-                a_raw[gu] = hh_pool.tile([P, S, 2048], BF16, name="a_raw", tag="hh")
+            if gu % 2 == 0 and s == 0:
+                a_raw[gu // 2] = hh_pool.tile([P, 4, 2048], BF16, name="a_raw", tag="hh256")
             nc.sync.dma_start(
-                out=a_raw[gu][:, s, :],
+                out=a_raw[gu // 2][:, 2 * (gu % 2) + s, :],
                 in_=support[s, 512 * (gu // 2) : 512 * (gu // 2 + 1), :].rearrange("(p h e) m -> h p (e m)", h=2, e=2)[gu % 2],
             )
 
+        load_a(0, 0)
+        load_a(1, 0)
         load_x(0)
         nc.sync.dma_start(out=eps_row[0:1, 0:1], in_=eps.rearrange("(o n) -> o n", o=1))
-        for gu in range(4):
-            for s in range(S):
-                load_a(s, gu)
-        for b in range(1, B):
-            load_x(b)
+        load_a(0, 1)
+        load_a(1, 1)
+        load_x(1)
+        load_a(0, 2)
+        load_a(1, 2)
+        load_a(0, 3)
+        load_a(1, 3)
+        load_x(2)
+        load_x(3)
 
         x_grp = {}
         x_codes = {}
@@ -101,7 +111,7 @@ def tile_ginconvfft_pa_t_kernel(tc, x, support, eps, out):
 
         def transpose_a(gu, engs):
             for s in range(S):
-                a32 = a_raw[gu][:, s, :].bitcast(F32)
+                a32 = a_raw[gu // 2][:, 2 * (gu % 2) + s, :].bitcast(F32)
                 grp = atg_pool.tile([P, 2048], BF16, name="at_grp", align_bytes=64)
                 g32 = grp[:].bitcast(F32)
                 for g in range(2):
@@ -182,7 +192,7 @@ def tile_ginconvfft_pa_t_kernel(tc, x, support, eps, out):
             b, c0, w, n_t = shape_of(ch)
             t0 = n_t * k % 4
             if t0 == 0:
-                hh[(ch, n_t * k // 4)] = hh_pool.tile([P, 4, 2, w, S], F32, name="hh", tag="hh")
+                hh[(ch, n_t * k // 4)] = hh_pool.tile([P, 4, 2, w, S], F32, name="hh", tag="hh%d" % w)
             for i in range(n_t):
                 nc.vector.scalar_tensor_tensor(
                     out=hh[(ch, n_t * k // 4)][:, t0 + i, 0, :, :],
@@ -223,72 +233,101 @@ def tile_ginconvfft_pa_t_kernel(tc, x, support, eps, out):
             h_codes[(ch, g)] = c
             h_scales[(ch, g)] = sc
 
-        def store(ch, k, eng):
-            b, c0, w, n_t = shape_of(ch)
-            g, t0 = n_t * k // 4, n_t * k % 4
-            o = o_pool.tile([P, n_t, 4 * w], F32, name="o")
-            copy(
-                eng,
-                o[:].rearrange("p i (f j) -> p i f j", j=2),
-                hh[(ch, g)][:, t0 : t0 + n_t, :, :, :].rearrange("p i j c s -> p i (c s) j"),
-            )
-            dst = out[b, 512 * g : 512 * (g + 1)].rearrange("(p t) l f -> p t (l f)", t=4)
-            nc.sync.dma_start(out=dst[:, t0 : t0 + n_t, 4 * c0 : 4 * (c0 + w)], in_=o[:])
+        o_tile = {}
+
+        def store(ch, k, eng, single):
+            g, t = k // 4, k % 4
+            if t % 2 == 0:
+                o_tile[ch] = o_pool.tile([P, 2, 4 * D], F32, name="o")
+            o = o_tile[ch]
+            copy(eng, o[:, t % 2, :].rearrange("p (f j) -> p f j", j=2), hh[(ch, g)][:, t, :, :, :].rearrange("p j c s -> p (c s) j"))
+            dst = out[ch, 512 * g : 512 * (g + 1)].rearrange("(p t) l f -> p t (l f)", t=4)
+            if single:
+                nc.sync.dma_start(out=dst[:, t, :], in_=o[:, t % 2, :])
+            elif t % 2 == 1:
+                nc.sync.dma_start(out=dst[:, t - 1 : t + 1, :], in_=o[:])
+
+        def pass1(i):
+            if i < 32:
+                mm1(i // 8, i % 8)
 
         def hop1(i):
-            add1(i // 4, i % 4)
+            add1(i // 8, i % 8)
 
-        regroup_x(0, "vv")
-        quant_x(0)
-        transpose_a(0, "ssss")
-        transpose_a(1, "ssss")
-        eps_bank = psum.tile([P, 512], F32, name="bank", tag="bank")
-        nc.tensor.matmul(out=eps_bank[:, 0:32], lhsT=ones[:], rhs=eps_row[:], start=True, stop=True)
-        gain = keep.tile([P, 1], F32, name="gain")
-        quant_a(0)
-        nc.vector.tensor_scalar_add(out=gain[:], in0=eps_bank[:, 0:1], scalar1=1.0)
-        mm1(0, 0)
-        transpose_a(2, "ssss")
-        quant_a(1)
-        hop1(0)
-        mm1(0, 1)
-        transpose_a(3, "ssss")
-        quant_a(2)
-        hop1(1)
-        regroup_h(0, 0, "gg")
-        mm1(0, 2)
-        quant_a(3)
-        hop1(2)
-        mm1(0, 3)
-        quant_h(0, 0)
-        mm1(1, 0)
-        hop1(3)
-        regroup_h(0, 1, "sg")
-        mm1(1, 1)
-        regroup_x(1, "ss")
-        hop1(4)
-        hop1(5)
-        regroup_h(1, 0, "sg")
-        quant_h(0, 1)
-        mm2(0, 0)
-        mm1(1, 2)
+        def quarter_x(b, n, eng):
+            if n == 0:
+                x_grp[b] = xg_pool.tile([P, 2, D, 4], BF16, name="x_grp", align_bytes=64)
+            g, cols = n // 2, slice(128 * (n % 2), 128 * (n % 2 + 1))
+            copy(eng, x_grp[b][:, g, cols, :], x_raw[b][:, 4 * g : 4 * (g + 1), cols].rearrange("p t d -> p d t"))
 
-        LEAD = 6
+        with tc.manual_schedule():
+            transpose_a(0, "ssss")
+            regroup_x(0, "vv")
+            quant_a(0)
+            quant_x(0)
+            eps_bank = psum.tile([P, 512], F32, name="bank", tag="bank")
+            nc.tensor.matmul(out=eps_bank[:, 0:32], lhsT=ones[:], rhs=eps_row[:], start=True, stop=True)
+            transpose_a(1, "ssss")
+            gain = keep.tile([P, 1], F32, name="gain")
+            nc.vector.tensor_scalar_add(out=gain[:], in0=eps_bank[:, 0:1], scalar1=1.0)
+            pass1(0)
+            pass1(1)
+            quant_a(1)
+            transpose_a(2, "ssss")
+            hop1(0)
+            hop1(1)
+            regroup_x(1, "vv")
+            transpose_a(3, "ssss")
+            pass1(2)
+            pass1(3)
+            quant_a(2)
+            quant_x(1)
+            pass1(4)
+            pass1(5)
+            hop1(2)
+            hop1(3)
+            regroup_h(0, 0, "gg")
+            quant_a(3)
+            pass1(6)
+            pass1(7)
+            hop1(4)
+            hop1(5)
+            hop1(6)
+            regroup_x(2, "ss")
+            hop1(7)
+            regroup_h(0, 1, "sg")
+            pass1(8)
+            pass1(9)
+            quant_h(0, 0)
+            hop1(8)
+            pass1(10)
+            hop1(9)
+            quant_x(2)
+            pass1(11)
+            quant_h(0, 1)
+            mm2(0, 0)
+            mm2(0, 1)
+            hop1(10)
+            pass1(12)
+
+        plan = {1: [11], 2: [12], 3: [13], 4: [14, 15]}
+        for i in range(16):
+            plan[i + 5] = [i + 16]
+        made = {}
         for i in range(32):
-            j = i + LEAD
-            if i % 2 == 1 and j - 3 < 32:
-                quant_h((j - 3) // 4, (j - 3) // 2 % 2)
-            if i in (1, 8, 16):
-                quant_x(1 + i // 8)
-            if i + 1 < 32:
-                mm2((i + 1) // 4, (i + 1) % 4)
-            if j + 1 < 32:
-                mm1((j + 1) // 4, (j + 1) % 4)
-            if j < 32:
+            add2(i // 8, i % 8)
+            store(i // 8, i % 8, ("sg" if i < 26 else "sv")[i % 2], i < 2 or i >= 30)
+            for j in plan.get(i, []):
                 hop1(j)
-                if j % 2 == 1:
-                    regroup_h(j // 4, j // 2 % 2, "sg")
-            add2(i // 4, i % 4)
-            store(i // 4, i % 4, ("sg" if j < 32 else "sv")[i % 2])
-            if i in (3, 11):
-                regroup_x(2 + i // 8, "sg")
+                pass1(j + 2)
+                if j % 4 == 3:
+                    regroup_h(j // 8, j // 4 % 2, "sg")
+                    made[i + 2] = (j // 8, j // 4 % 2)
+            if i in made:
+                quant_h(made[i][0], made[i][1])
+            if i == 8:
+                quant_x(3)
+            if i + 2 < 32:
+                mm2((i + 2) // 8, (i + 2) % 8)
+            if i % 2 == 1 and i < 8:
+                quarter_x(3, i // 2, "s")

@@ -48,7 +48,7 @@ def tile_ginconvfft_pa_t_kernel(tc, x, support, eps, out):
 
         eps_row = keep.tile([P, 32], BF16, name="eps_row")
         nc.vector.memset(eps_row[:], 0.0)
-        ones = keep.tile([P, P], BF16, name="ones")
+        ones = keep.tile([P, 512], BF16, name="ones")
         nc.vector.memset(ones[:], 1.0)
         ident = keep.tile([P, P], F32, name="ident")
         make_identity(nc, ident[:])
@@ -261,12 +261,19 @@ def tile_ginconvfft_pa_t_kernel(tc, x, support, eps, out):
             copy(eng, x_grp[b][:, g, cols, :], x_raw[b][:, 4 * g : 4 * (g + 1), cols].rearrange("p t d -> p d t"))
 
         with tc.manual_schedule():
+            eps_bank = psum.tile([P, 512], F32, name="bank", tag="bank")
+
+            def warm(times):
+                for i in range(times):
+                    nc.tensor.matmul(out=eps_bank[:], lhsT=ones[:, 0:P], rhs=ones[:], start=True, stop=True)
+
+            warm(5)
             transpose_a(0, "ssss")
+            warm(2)
             regroup_x(0, "vv")
             quant_a(0)
             quant_x(0)
-            eps_bank = psum.tile([P, 512], F32, name="bank", tag="bank")
-            nc.tensor.matmul(out=eps_bank[:, 0:32], lhsT=ones[:], rhs=eps_row[:], start=True, stop=True)
+            nc.tensor.matmul(out=eps_bank[:, 0:32], lhsT=ones[:, 0:P], rhs=eps_row[:], start=True, stop=True)
             transpose_a(1, "ssss")
             gain = keep.tile([P, 1], F32, name="gain")
             nc.vector.tensor_scalar_add(out=gain[:], in0=eps_bank[:, 0:1], scalar1=1.0)

@@ -284,9 +284,9 @@ def tile_ginconvfft_pa_t_kernel(tc, x, support, eps, out):
             hop1(0)
             hop1(1)
             regroup_x(1, "vv")
-            transpose_a(3, "ssss")
             pass1(2)
             pass1(3)
+            transpose_a(3, "ssss")
             quant_a(2)
             quant_x(1)
             pass1(4)
@@ -328,8 +328,8 @@ def tile_ginconvfft_pa_t_kernel(tc, x, support, eps, out):
                 hop1(j)
                 pass1(j + 2)
                 if j % 4 == 3:
-                    regroup_h(j // 8, j // 4 % 2, "sg")
-                    made[i + 2] = (j // 8, j // 4 % 2)
+                    regroup_h(j // 8, j // 4 % 2, "sg" if j % 8 == 7 else "ss")
+                    made[i + (2 if j % 8 == 7 else 3)] = (j // 8, j // 4 % 2)
             if i in made:
                 quant_h(made[i][0], made[i][1])
             if i == 8:

@@ -46,6 +46,12 @@ def tile_ginconvfft_pa_t_kernel(tc, x, support, eps, out):
                     d, f = (dst[:, part], src[:, part]) if axis == 1 else (dst[:, :, part], src[:, :, part])
                     nc.gpsimd.tensor_scalar(out=d, in0=f, scalar1=1.0, scalar2=0.0, op0=MULT, op1=ADD)
 
+        def copy_rows(eng, dst, src):
+            if eng == "g":
+                copy(eng, dst, src.rearrange("p t c -> p c t"))
+            else:
+                copy(eng, dst.rearrange("p (c i) t -> p c t i", i=4), src.rearrange("p t (c i) -> p c t i", i=4))
+
         eps_row = keep.tile([P, 32], BF16, name="eps_row")
         nc.vector.memset(eps_row[:], 0.0)
         ones = keep.tile([P, 512], BF16, name="ones")
@@ -93,7 +99,7 @@ def tile_ginconvfft_pa_t_kernel(tc, x, support, eps, out):
         def regroup_x(b, engs):
             t = xg_pool.tile([P, 2, D, 4], BF16, name="x_grp", align_bytes=64)
             for g in range(2):
-                copy(engs[g], t[:, g, :, :], x_raw[b][:, 4 * g : 4 * (g + 1), :].rearrange("p t d -> p d t"))
+                copy_rows(engs[g], t[:, g, :, :], x_raw[b][:, 4 * g : 4 * (g + 1), :])
             x_grp[b] = t
 
         def quant_x(b):
@@ -220,7 +226,7 @@ def tile_ginconvfft_pa_t_kernel(tc, x, support, eps, out):
             b, c0, w, n_t = shape_of(ch)
             grp = hg_pool.tile([P, S, w, 4], BF16, name="h_grp", align_bytes=64, tag="hg%d" % w)
             for s in range(S):
-                copy(engs[s], grp[:, s, :, :], hh[(ch, g)][:, :, 0, :, s].rearrange("p t c -> p c t"))
+                copy_rows(engs[s], grp[:, s, :, :], hh[(ch, g)][:, :, 0, :, s])
             h_grp[(ch, g)] = grp
 
         def quant_h(ch, g):
@@ -258,7 +264,7 @@ def tile_ginconvfft_pa_t_kernel(tc, x, support, eps, out):
             if n == 0:
                 x_grp[b] = xg_pool.tile([P, 2, D, 4], BF16, name="x_grp", align_bytes=64)
             g, cols = n // 2, slice(128 * (n % 2), 128 * (n % 2 + 1))
-            copy(eng, x_grp[b][:, g, cols, :], x_raw[b][:, 4 * g : 4 * (g + 1), cols].rearrange("p t d -> p d t"))
+            copy_rows(eng, x_grp[b][:, g, cols, :], x_raw[b][:, 4 * g : 4 * (g + 1), cols])
 
         with tc.manual_schedule():
             eps_bank = psum.tile([P, 512], F32, name="bank", tag="bank")

from contextlib import ExitStack

import concourse.mybir as mybir
from concourse.masks import make_identity

F32 = mybir.dt.float32
BF16 = mybir.dt.bfloat16
U32 = mybir.dt.uint32
U8 = mybir.dt.uint8
FP8X4 = mybir.dt.float8_e4m3fn_x4
MULT = mybir.AluOpType.mult
ADD = mybir.AluOpType.add

P = 128
B = 4
D = 256
S = 2
NT = 8
FLOPS = 4 * 2 * 1024 * 1024 * 1024

CHUNKS = [(b, 0, 256) for b in range(4)]


def tile_ginconvfft_pa_t_kernel(tc, x, support, eps, out):
    nc = tc.nc
    with ExitStack() as ctx:
        keep = ctx.enter_context(tc.tile_pool(name="keep", bufs=1))
        atg_pool = ctx.enter_context(tc.tile_pool(name="atg", bufs=4))
        xg_pool = ctx.enter_context(tc.tile_pool(name="xg", bufs=2))
        hh_pool = ctx.enter_context(tc.tile_pool(name="hh", bufs=6))
        hg_pool = ctx.enter_context(tc.tile_pool(name="hg", bufs=2))
        hc_pool = ctx.enter_context(tc.tile_pool(name="hc", bufs=4))
        o_pool = ctx.enter_context(tc.tile_pool(name="o", bufs=5))
        psum = ctx.enter_context(tc.psum_pool(name="psum", bufs=8))

        def copy(eng, dst, src):
            if eng == "v":
                nc.vector.tensor_copy(out=dst, in_=src)
            elif eng == "s":
                nc.scalar.copy(out=dst, in_=src)
            else:
                axis = 1 if dst.shape[1] > 2 else 2
                n = dst.shape[axis] // 2
                for i in range(2):
                    part = slice(i * n, (i + 1) * n)
                    d, f = (dst[:, part], src[:, part]) if axis == 1 else (dst[:, :, part], src[:, :, part])
                    nc.gpsimd.tensor_scalar(out=d, in0=f, scalar1=1.0, scalar2=0.0, op0=MULT, op1=ADD)

        def copy_rows(eng, dst, src):
            if eng == "g":
                copy(eng, dst, src.rearrange("p t c -> p c t"))
            else:
                copy(eng, dst.rearrange("p (c i) t -> p c t i", i=4), src.rearrange("p t (c i) -> p c t i", i=4))

        eps_row = keep.tile([P, 32], BF16, name="eps_row")
        nc.vector.memset(eps_row[:], 0.0)
        ones = keep.tile([P, 512], BF16, name="ones")
        nc.vector.memset(ones[:], 1.0)
        ident = keep.tile([P, P], F32, name="ident")
        make_identity(nc, ident[:])

        x_raw = {}
        a_raw = {}

        def load_x(b):
            t = keep.tile([P, NT, D], BF16, name="x_raw%d" % b)
            nc.sync.dma_start(
                out=t[:].rearrange("p (g t) d -> p g (t d)", t=4),
                in_=x[b].rearrange("(g p t) l h -> p g (t l h)", g=2, p=P, t=4),
            )
            x_raw[b] = t

        def load_a(s, gu):
            if gu % 2 == 0 and s == 0:
                a_raw[gu // 2] = hh_pool.tile([P, 4, 2048], BF16, name="a_raw", tag="hh256")
            nc.sync.dma_start(
                out=a_raw[gu // 2][:, 2 * (gu % 2) + s, :],
                in_=support[s, 512 * (gu // 2) : 512 * (gu // 2 + 1), :].rearrange("(p h e) m -> h p (e m)", h=2, e=2)[gu % 2],
            )

        load_a(0, 0)
        load_a(1, 0)
        load_x(0)
        nc.sync.dma_start(out=eps_row[0:1, 0:1], in_=eps.rearrange("(o n) -> o n", o=1))
        load_a(0, 1)
        load_a(1, 1)
        load_x(1)
        load_a(0, 2)
        load_a(1, 2)
        load_a(0, 3)
        load_a(1, 3)
        load_x(2)
        load_x(3)

        x_grp = {}
        x_codes = {}
        x_scales = {}

        def regroup_x(b, engs):
            t = xg_pool.tile([P, 2, D, 4], BF16, name="x_grp", align_bytes=64)
            for g in range(2):
                copy_rows(engs[g], t[:, g, :, :], x_raw[b][:, 4 * g : 4 * (g + 1), :])
            x_grp[b] = t

        def quant_x(b):
            c = keep.tile([P, 512], U32, name="x_codes%d" % b, align_bytes=64)
            sc = keep.tile([P, 512], U8, name="x_scales%d" % b, align_bytes=64)
            nc.vector.quantize_mx(
                out=c[:].bitcast(FP8X4), scales=sc[:], in_=x_grp[b][:].rearrange("p g d t -> p (g d t)")
            )
            x_codes[b] = c
            x_scales[b] = sc

        at_grp = {}
        at_codes = {}
        at_scales = {}

        def transpose_a(gu, engs):
            for s in range(S):
                a32 = a_raw[gu // 2][:, 2 * (gu % 2) + s, :].bitcast(F32)
                grp = atg_pool.tile([P, 2048], BF16, name="at_grp", align_bytes=64)
                g32 = grp[:].bitcast(F32)
                for g in range(2):
                    bank = psum.tile([P, 512], F32, name="bank", tag="bank")
                    for u in range(2):
                        for e in range(2):
                            w0 = 512 * e + 256 * g
                            nc.tensor.transpose(
                                out=bank[:, 256 * u + 128 * e : 256 * u + 128 * (e + 1)],
                                in_=a32[:, w0 + u : w0 + 256 : 2],
                                identity=ident[:],
                            )
                    copy(
                        engs[2 * s + g],
                        g32[:, 512 * g : 512 * (g + 1)].rearrange("p (w u) -> p w u", u=2),
                        bank[:].rearrange("p (u w) -> p w u", u=2),
                    )
                at_grp[(s, gu)] = grp

        def quant_a(gu):
            for s in range(S):
                c = keep.tile([P, 512], U32, name="at_codes%d_%d" % (s, gu), align_bytes=64)
                sc = keep.tile([P, 512], U8, name="at_scales%d_%d" % (s, gu), align_bytes=64)
                nc.vector.quantize_mx(out=c[:].bitcast(FP8X4), scales=sc[:], in_=at_grp[(s, gu)][:])
                at_codes[(s, gu)] = c
                at_scales[(s, gu)] = sc

        hh = {}
        h_grp = {}
        h_codes = {}
        h_scales = {}
        banks = {}

        def shape_of(ch):
            b, c0, w = CHUNKS[ch]
            return b, c0, w, 256 // w

        def mx_bank(ch, k, rhs_of):
            b, c0, w, n_t = shape_of(ch)
            bank = psum.tile([P, 512], F32, name="bank", tag="bank")
            for i in range(n_t):
                nt = n_t * k + i
                gu, e = nt // 2, nt % 2
                for s in range(S):
                    for g in range(2):
                        cols = slice(256 * g + 128 * e, 256 * g + 128 * (e + 1))
                        rc, rs = rhs_of(s, g)
                        nc.tensor.matmul_mx(
                            out=bank[:, w * (n_t * s + i) : w * (n_t * s + i + 1)],
                            lhsT=at_codes[(s, gu)][:, cols].bitcast(FP8X4),
                            lhsT_scale=at_scales[(s, gu)][:, cols],
                            rhs=rc.bitcast(FP8X4),
                            rhs_scale=rs,
                            start=(g == 0),
                            stop=(g == 1),
                        )
            return bank

        def mm1(ch, k):
            b, c0, w, n_t = shape_of(ch)

            def rhs_of(s, g):
                cols = slice(D * g + c0, D * g + c0 + w)
                return x_codes[b][:, cols], x_scales[b][:, cols]

            banks[(1, ch, k)] = mx_bank(ch, k, rhs_of)

        def mm2(ch, k):
            b, c0, w, n_t = shape_of(ch)

            def rhs_of(s, g):
                cols = slice(w * s, w * (s + 1))
                return h_codes[(ch, g)][:, cols], h_scales[(ch, g)][:, cols]

            banks[(2, ch, k)] = mx_bank(ch, k, rhs_of)

        def add1(ch, k):
            b, c0, w, n_t = shape_of(ch)
            t0 = n_t * k % 4
            if t0 == 0:
                hh[(ch, n_t * k // 4)] = hh_pool.tile([P, 4, 2, w, S], F32, name="hh", tag="hh%d" % w)
            for i in range(n_t):
                nc.vector.scalar_tensor_tensor(
                    out=hh[(ch, n_t * k // 4)][:, t0 + i, 0, :, :],
                    in0=x_raw[b][:, n_t * k + i, c0 : c0 + w].unsqueeze(2).to_broadcast([P, w, S]),
                    scalar=gain[:, 0:1],
                    in1=banks[(1, ch, k)][:].rearrange("p (s i c) -> p i c s", s=S, c=w)[:, i, :, :],
                    op0=MULT,
                    op1=ADD,
                )

        def add2(ch, k):
            b, c0, w, n_t = shape_of(ch)
            t0 = n_t * k % 4
            tl = hh[(ch, n_t * k // 4)]
            nc.vector.scalar_tensor_tensor(
                out=tl[:, t0 : t0 + n_t, 1, :, :],
                in0=tl[:, t0 : t0 + n_t, 0, :, :],
                scalar=gain[:, 0:1],
                in1=banks[(2, ch, k)][:].rearrange("p (s i c) -> p i c s", s=S, c=w),
                op0=MULT,
                op1=ADD,
            )

        def regroup_h(ch, g, engs):
            b, c0, w, n_t = shape_of(ch)
            grp = hg_pool.tile([P, S, w, 4], BF16, name="h_grp", align_bytes=64, tag="hg%d" % w)
            for s in range(S):
                copy_rows(engs[s], grp[:, s, :, :], hh[(ch, g)][:, :, 0, :, s])
            h_grp[(ch, g)] = grp

        def quant_h(ch, g):
            b, c0, w, n_t = shape_of(ch)
            c = hc_pool.tile([P, S * w], U32, name="h_codes", align_bytes=64, tag="hc%d" % w)
            sc = hc_pool.tile([P, S * w], U8, name="h_scales", align_bytes=64, tag="hs%d" % w)
            nc.vector.quantize_mx(
                out=c[:].bitcast(FP8X4), scales=sc[:], in_=h_grp[(ch, g)][:].rearrange("p s c t -> p (s c t)")
            )
            h_codes[(ch, g)] = c
            h_scales[(ch, g)] = sc

        o_tile = {}

        def store(ch, k, eng, single):
            g, t = k // 4, k % 4
            if t % 2 == 0:
                o_tile[ch] = o_pool.tile([P, 2, 4 * D], F32, name="o")
            o = o_tile[ch]
            copy(eng, o[:, t % 2, :].rearrange("p (f j) -> p f j", j=2), hh[(ch, g)][:, t, :, :, :].rearrange("p j c s -> p (c s) j"))
            dst = out[ch, 512 * g : 512 * (g + 1)].rearrange("(p t) l f -> p t (l f)", t=4)
            if single:
                nc.sync.dma_start(out=dst[:, t, :], in_=o[:, t % 2, :])
            elif t % 2 == 1:
                nc.sync.dma_start(out=dst[:, t - 1 : t + 1, :], in_=o[:])

        def pass1(i):
            if i < 32:
                mm1(i // 8, i % 8)

        def hop1(i):
            add1(i // 8, i % 8)

        def quarter_x(b, n, eng):
            if n == 0:
                x_grp[b] = xg_pool.tile([P, 2, D, 4], BF16, name="x_grp", align_bytes=64)
            g, cols = n // 2, slice(128 * (n % 2), 128 * (n % 2 + 1))
            copy_rows(eng, x_grp[b][:, g, cols, :], x_raw[b][:, 4 * g : 4 * (g + 1), cols])

        with tc.manual_schedule():
            eps_bank = psum.tile([P, 512], F32, name="bank", tag="bank")

            def warm(times):
                for i in range(times):
                    nc.tensor.matmul(out=eps_bank[:], lhsT=ones[:, 0:P], rhs=ones[:], start=True, stop=True)

            warm(5)
            transpose_a(0, "ssss")
            warm(2)
            regroup_x(0, "vv")
            quant_a(0)
            quant_x(0)
            nc.tensor.matmul(out=eps_bank[:, 0:32], lhsT=ones[:, 0:P], rhs=eps_row[:], start=True, stop=True)
            transpose_a(1, "ssss")
            gain = keep.tile([P, 1], F32, name="gain")
            nc.vector.tensor_scalar_add(out=gain[:], in0=eps_bank[:, 0:1], scalar1=1.0)
            pass1(0)
            pass1(1)
            quant_a(1)
            transpose_a(2, "ssss")
            hop1(0)
            hop1(1)
            regroup_x(1, "vv")
            pass1(2)
            pass1(3)
            transpose_a(3, "ssss")
            quant_a(2)
            quant_x(1)
            pass1(4)
            pass1(5)
            hop1(2)
            hop1(3)
            regroup_h(0, 0, "gg")
            quant_a(3)
            pass1(6)
            pass1(7)
            hop1(4)
            hop1(5)
            hop1(6)
            regroup_x(2, "ss")
            hop1(7)
            regroup_h(0, 1, "sg")
            pass1(8)
            pass1(9)
            quant_h(0, 0)
            hop1(8)
            pass1(10)
            hop1(9)
            quant_x(2)
            pass1(11)
            quant_h(0, 1)
            mm2(0, 0)
            mm2(0, 1)
            hop1(10)
            pass1(12)

        plan = {1: [11], 2: [12], 3: [13], 4: [14, 15]}
        for i in range(16):
            plan[i + 5] = [i + 16]
        made = {}
        for i in range(32):
            add2(i // 8, i % 8)
            store(i // 8, i % 8, ("sg" if i < 26 else "sv")[i % 2], i < 2 or i >= 30)
            for j in plan.get(i, []):
                hop1(j)
                pass1(j + 2)
                if j % 4 == 3:
                    regroup_h(j // 8, j // 4 % 2, "sg" if j % 8 == 7 else "ss")
                    made[i + (2 if j % 8 == 7 else 3)] = (j // 8, j // 4 % 2)
            if i in made:
                quant_h(made[i][0], made[i][1])
            if i == 8:
                quant_x(3)
            if i + 2 < 32:
                mm2((i + 2) // 8, (i + 2) % 8)
            if i % 2 == 1 and i < 8:
                quarter_x(3, i // 2, "s")
